import numpy as np
import ml_dtypes


def mxq(x, axis, fmt="e4m3"):
    dtype, down = {"e4m3": (ml_dtypes.float8_e4m3fn, 7), "e5m2": (ml_dtypes.float8_e5m2, 14)}[fmt]
    v = np.moveaxis(np.asarray(x, np.float32).astype(ml_dtypes.bfloat16).astype(np.float64), axis, -1)
    blocks = v.reshape(v.shape[:-1] + (-1, 32))
    amax = np.abs(blocks).max(-1, keepdims=True)
    byte = np.maximum(np.where(amax > 0, np.frexp(amax)[1] - 1 + 127, 0) - down, 1)
    scale = np.exp2(byte - 127.0)
    codes = (blocks / scale).astype(np.float32).astype(dtype).astype(np.float64)
    return np.moveaxis((codes * scale).reshape(v.shape), -1, axis)


WIDE = False


def mx_kscale(k):
    if not WIDE:
        return np.ones(k)
    levels = np.array([10, -10, 5, -5, 0])
    a = np.random.permutation(np.resize(levels, k // 512 * 4)).reshape(k // 512, 4)
    idx = np.arange(k)
    return np.exp2(a[idx // 512, idx % 128 // 32])


BF16 = ml_dtypes.bfloat16


def bf(x):
    return np.asarray(x, np.float32).astype(BF16)


def f64(x):
    return np.asarray(x).astype(np.float64)


E2M1 = np.array([0.0, 0.5, 1.0, 1.5, 2.0, 3.0, 4.0, 6.0, -0.0, -0.5, -1.0, -1.5, -2.0, -3.0, -4.0, -6.0])


def pack_weight(w, fmt):
    k, n = w.shape
    w = f64(bf(w)).reshape(k // 32, 32, n)
    amax = np.abs(w).max(1)
    if fmt == "e4m3":
        byte = np.frexp(amax)[1] - 1 + 127 - 7
    else:
        mant, ex = np.frexp(amax / 6.0)
        byte = np.where(mant > 0.5, ex, ex - 1) + 127
    byte = np.clip(np.where(amax > 0, byte, 1), 1, 254)
    scaled = (w * np.exp2(127.0 - byte)[:, None, :]).reshape(k, n).astype(np.float32)
    by_word = np.ascontiguousarray(scaled.reshape(k // 512, 128, 4, n).transpose(0, 1, 3, 2))
    if fmt == "e4m3":
        words = by_word.astype(ml_dtypes.float8_e4m3fn).view(np.uint8)
    else:
        c = by_word.astype(ml_dtypes.float4_e2m1fn).view(np.uint8) & 0xF
        words = c[..., 0::2] | (c[..., 1::2] << 4)
    return np.ascontiguousarray(words), np.ascontiguousarray(byte.astype(np.uint8).reshape(k // 512, 16, n))


def unpack_weight(words, scales, fmt):
    g, p, n, _ = words.shape
    if fmt == "e4m3":
        vals = np.ascontiguousarray(words).view(ml_dtypes.float8_e4m3fn).astype(np.float64)
    else:
        nib = np.empty((g, p, n, 4), np.uint8)
        nib[..., 0::2] = words & 0xF
        nib[..., 1::2] = words >> 4
        vals = E2M1[nib]
    vals = vals * np.repeat(np.exp2(scales.astype(np.float64) - 127.0), 8, axis=1)[..., None]
    return vals.transpose(0, 1, 3, 2).reshape(g * 512, n)


B, T, D, H, HKV, HD, R, DFF = 1, 128, 8192, 16, 8, 128, 128, 6144
HALF = HD // 2
EPS = 1e-6
THETA = 1e6
FMT = "e4m3"


def rms_norm(x, w):
    return x / np.sqrt(np.mean(x * x, axis=-1, keepdims=True) + EPS) * w


def rotate_half(x):
    return np.concatenate([-x[..., HALF:], x[..., :HALF]], axis=-1)


def setup_inputs():
    rn = np.random.standard_normal
    s = mx_kscale(D)
    inv_freq = 1.0 / THETA ** (np.arange(HALF) / HALF)
    freqs = np.arange(T)[:, None] * inv_freq[None, :]
    emb = np.concatenate([freqs, freqs], axis=-1)
    hidden_states = bf(rn((B, T, D)) * np.exp(0.5 * rn((B, T, 1))))
    ln1_w = bf((1.0 + 0.1 * rn(D)) * s)
    Wq_words, Wq_scales = pack_weight(rn((D, H * HD)) / np.sqrt(D) / s[:, None], FMT)
    Wk_words, Wk_scales = pack_weight(rn((D, HKV * HD)) / np.sqrt(D) / s[:, None], FMT)
    Wv_words, Wv_scales = pack_weight(rn((D, HKV * HD)) / np.sqrt(D) / s[:, None], FMT)
    q_norm_w = bf(1.0 + 0.1 * rn(HD))
    k_norm_w = bf(1.0 + 0.1 * rn(HD))
    return {
        "hidden_states": hidden_states,
        "ln1_w": ln1_w,
        "Wq_words": Wq_words,
        "Wq_scales": Wq_scales,
        "Wk_words": Wk_words,
        "Wk_scales": Wk_scales,
        "Wv_words": Wv_words,
        "Wv_scales": Wv_scales,
        "q_norm_w": q_norm_w,
        "k_norm_w": k_norm_w,
        "cos": bf(np.cos(emb)),
        "sin": bf(np.sin(emb)),
    }


def reference(hidden_states, ln1_w, Wq_words, Wq_scales, Wk_words, Wk_scales, Wv_words, Wv_scales, q_norm_w, k_norm_w, cos, sin):
    h = rms_norm(f64(hidden_states), f64(ln1_w))
    hq = mxq(h, 2, "e4m3")
    q = rms_norm((hq @ unpack_weight(Wq_words, Wq_scales, FMT)).reshape(B, T, H, HD), f64(q_norm_w)).transpose(0, 2, 1, 3)
    k = rms_norm((hq @ unpack_weight(Wk_words, Wk_scales, FMT)).reshape(B, T, HKV, HD), f64(k_norm_w)).transpose(0, 2, 1, 3)
    v = (hq @ unpack_weight(Wv_words, Wv_scales, FMT)).reshape(B, T, HKV, HD).transpose(0, 2, 1, 3)
    c, s_ = f64(cos)[None, None], f64(sin)[None, None]
    q = q * c + rotate_half(q) * s_
    k = k * c + rotate_half(k) * s_
    return q, k, v

@@ -1,0 +1,236 @@
+from contextlib import ExitStack
+
+import concourse.mybir as mybir
+from concourse.masks import make_identity
+
+BF16 = mybir.dt.bfloat16
+F32 = mybir.dt.float32
+I32 = mybir.dt.int32
+U8 = mybir.dt.uint8
+U32 = mybir.dt.uint32
+FP8X4 = mybir.dt.float8_e4m3fn_x4
+MULT = mybir.AluOpType.mult
+ADD = mybir.AluOpType.add
+SQUARE = mybir.ActivationFunctionType.Square
+COPY = mybir.ActivationFunctionType.Copy
+
+P = 128
+D = 8192
+PACK = 4
+GROUP = P * PACK
+GROUPS = D // GROUP
+HEAD = 128
+HALF = HEAD // 2
+BANK = 512
+HEADS_PER_BANK = BANK // HEAD
+N_Q, N_K, N_V = 2048, 1024, 1024
+EPS = 1e-6
+SHARED = 4
+QUADRANT = 32
+X_CHUNKS = 4
+LOAD_BYTES = 8192
+WORD_BUFFERS = 14
+
+FLOPS = 2 * P * D * (N_Q + N_K + N_V)
+
+
+def inverse_rms(nc, pool, sum_sq, count):
+    width = sum_sq.shape[1]
+    mean_sq = pool.tile([P, width], F32, name="mean_sq")
+    nc.vector.tensor_scalar(out=mean_sq[:], in0=sum_sq, scalar1=1.0 / count, scalar2=EPS, op0=MULT, op1=ADD)
+    rms = pool.tile([P, width], F32, name="rms")
+    nc.scalar.sqrt(rms[:], mean_sq[:])
+    inv = pool.tile([P, width], F32, name="inv")
+    nc.vector.reciprocal(inv[:], rms[:])
+    return inv
+
+
+def load_scale_planes(nc, pool, w_scales, n, name):
+    planes = pool.tile([P, GROUPS // SHARED, n], U8, name=name, align_bytes=64)
+    nc.vector.memset(planes[:].bitcast(I32), 0)
+    for s in range(GROUPS // SHARED):
+        for quad in range(P // QUADRANT):
+            nc.sync.dma_start(
+                out=planes[QUADRANT * quad : QUADRANT * quad + SHARED * PACK, s, :].bitcast(I32),
+                in_=w_scales[SHARED * s : SHARED * (s + 1), PACK * quad : PACK * (quad + 1), :].bitcast(I32),
+            )
+    return planes
+
+
+def rope_tables(nc, pool, gain, cos_sb, sin_sb, name):
+    cos_gain = pool.tile([P, HEAD], F32, name=name + "_cos_gain")
+    nc.vector.tensor_tensor(out=cos_gain[:], in0=gain, in1=cos_sb[:], op=MULT)
+    sin_gain = pool.tile([P, HEAD], F32, name=name + "_sin_gain")
+    nc.vector.scalar_tensor_tensor(
+        out=sin_gain[:, 0:HALF], in0=gain[:, HALF:HEAD], scalar=-1.0, in1=sin_sb[:, 0:HALF], op0=MULT, op1=MULT
+    )
+    nc.vector.tensor_tensor(out=sin_gain[:, HALF:HEAD], in0=gain[:, 0:HALF], in1=sin_sb[:, HALF:HEAD], op=MULT)
+    return cos_gain, sin_gain
+
+
+def tile_rawkvinjector_pa_k_kernel(
+    tc,
+    hidden_states,
+    ln1_w,
+    Wq_words,
+    Wq_scales,
+    Wk_words,
+    Wk_scales,
+    Wv_words,
+    Wv_scales,
+    q_norm_w,
+    k_norm_w,
+    cos,
+    sin,
+    out_0,
+    out_1,
+    out_2,
+):
+    nc = tc.nc
+    with ExitStack() as ctx:
+        ctx.enter_context(tc.manual_schedule())
+        keep = ctx.enter_context(tc.tile_pool(name="keep", bufs=1))
+        small = ctx.enter_context(tc.tile_pool(name="small", bufs=2))
+        stage = ctx.enter_context(tc.tile_pool(name="stage", bufs=2))
+        stream = ctx.enter_context(tc.tile_pool(name="stream", bufs=WORD_BUFFERS))
+        psum = ctx.enter_context(tc.psum_pool(name="psum", bufs=8))
+
+        x = keep.tile([P, D], BF16, name="x")
+        chunk = D // X_CHUNKS
+        for c in range(X_CHUNKS):
+            cols = slice(c * chunk, (c + 1) * chunk)
+            nc.sync.dma_start(out=x[:, cols], in_=hidden_states[0][:, cols])
+
+        cos_sb = keep.tile([P, HEAD], BF16, name="cos_sb")
+        nc.scalar.dma_start(out=cos_sb[:], in_=cos)
+        sin_sb = keep.tile([P, HEAD], BF16, name="sin_sb")
+        nc.scalar.dma_start(out=sin_sb[:], in_=sin)
+
+        gains = keep.tile([P, D + 2 * HEAD], BF16, name="gains")
+        nc.vector.memset(gains[:].bitcast(I32), 0)
+        nc.scalar.dma_start(out=gains[0:1, 0:D], in_=ln1_w.unsqueeze(0))
+        nc.scalar.dma_start(out=gains[0:1, D : D + HEAD], in_=q_norm_w.unsqueeze(0))
+        nc.scalar.dma_start(out=gains[0:1, D + HEAD : D + 2 * HEAD], in_=k_norm_w.unsqueeze(0))
+        ones = keep.tile([P, P], BF16, name="ones")
+        nc.gpsimd.memset(ones[:], 1.0)
+        ident = keep.tile([P, P], BF16, name="ident")
+        make_identity(nc, ident[:])
+
+        q_planes = load_scale_planes(nc, keep, Wq_scales, N_Q, "q_planes")
+        k_planes = load_scale_planes(nc, keep, Wk_scales, N_K, "k_planes")
+        v_planes = load_scale_planes(nc, keep, Wv_scales, N_V, "v_planes")
+
+        chunk_sums = small.tile([P, X_CHUNKS], F32, name="chunk_sums")
+        for c in range(X_CHUNKS):
+            squares = stage.tile([P, chunk], BF16, name="squares")
+            nc.scalar.activation(
+                out=squares[:], in_=x[:, c * chunk : (c + 1) * chunk], func=SQUARE, accum_out=chunk_sums[:, c : c + 1]
+            )
+        row_sum = small.tile([P, 1], F32, name="row_sum")
+        nc.vector.tensor_reduce(out=row_sum[:], in_=chunk_sums[:], axis=mybir.AxisListType.X, op=ADD)
+        inv_rms_x = inverse_rms(nc, small, row_sum[:], D)
+
+        h = keep.tile([P, D], BF16, name="h")
+        for g in range(GROUPS):
+            cols = slice(g * GROUP, (g + 1) * GROUP)
+            ln1_everywhere = psum.tile([P, GROUP], F32, name="ln1_everywhere", tag="bank")
+            nc.tensor.matmul(out=ln1_everywhere[:], lhsT=ones[:], rhs=gains[:, cols], start=True, stop=True)
+            nc.vector.scalar_tensor_tensor(
+                out=h[:, cols], in0=x[:, cols], scalar=inv_rms_x[:, 0:1], in1=ln1_everywhere[:], op0=MULT, op1=MULT
+            )
+
+        h_codes = keep.tile([P, GROUPS * P], U32, name="h_codes", align_bytes=64)
+        h_planes = keep.tile([P, GROUPS * P], U8, name="h_planes", align_bytes=64)
+        pair = 2
+        for first in range(0, GROUPS, pair):
+            h_t = psum.tile([P, pair, PACK, P], BF16, name="h_t", tag="bank")
+            for i in range(pair):
+                g = first + i
+                for t in range(PACK):
+                    nc.tensor.transpose(h_t[:, i, t, :], h[:, g * GROUP + t : (g + 1) * GROUP : PACK], ident[:])
+            grouped = stage.tile([P, pair, P, PACK], BF16, name="grouped", align_bytes=64)
+            nc.scalar.copy(out=grouped[:], in_=h_t[:].rearrange("p i t r -> p i r t"))
+            cols = slice(first * P, (first + pair) * P)
+            nc.vector.quantize_mx(
+                out=h_codes[:, cols].bitcast(FP8X4),
+                scales=h_planes[:, cols],
+                in_=grouped[:].rearrange("p i r t -> p (i r t)"),
+            )
+
+        head_gains = psum.tile([P, 2 * HEAD], F32, name="head_gains", tag="bank")
+        nc.tensor.matmul(out=head_gains[:], lhsT=ones[:], rhs=gains[:, D : D + 2 * HEAD], start=True, stop=True)
+        q_tables = rope_tables(nc, keep, head_gains[:, 0:HEAD], cos_sb, sin_sb, "q")
+        k_tables = rope_tables(nc, keep, head_gains[:, HEAD : 2 * HEAD], cos_sb, sin_sb, "k")
+
+        def project(w_words, planes, n):
+            sums = [psum.tile([P, BANK], F32, name="sums", tag="bank") for bank in range(n // BANK)]
+            per_load = LOAD_BYTES // (n * PACK)
+            for first in range(0, GROUPS, per_load):
+                words = stream.tile([P, per_load, n * PACK], U8, name="words", align_bytes=64)
+                nc.sync.dma_start(
+                    out=words[:].bitcast(I32),
+                    in_=w_words[first : first + per_load].rearrange("g p n t -> p g (n t)").bitcast(I32),
+                )
+                for i in range(per_load):
+                    g = first + i
+                    for bank in range(n // BANK):
+                        nc.tensor.matmul_mx(
+                            out=sums[bank][:],
+                            lhsT=h_codes[:, g * P : (g + 1) * P].bitcast(FP8X4),
+                            lhsT_scale=h_planes[:, g * P : (g + 1) * P],
+                            rhs=words[:, i, bank * BANK * PACK : (bank + 1) * BANK * PACK].bitcast(FP8X4),
+                            rhs_scale=planes[PACK * (g % SHARED) : P, g // SHARED, bank * BANK : (bank + 1) * BANK],
+                            start=(g == 0),
+                            stop=(g == GROUPS - 1),
+                        )
+            return sums
+
+        def norm_rope_store(sums, tables, out_heads):
+            cos_gain, sin_gain = tables
+            u = stage.tile([P, HEADS_PER_BANK, HEAD], F32, name="u")
+            nc.scalar.copy(out=u[:].rearrange("p h d -> p (h d)"), in_=sums[:])
+            sum_sq = small.tile([P, HEADS_PER_BANK], F32, name="sum_sq")
+            for head in range(HEADS_PER_BANK):
+                head_squares = stage.tile([P, HEAD], F32, name="head_squares")
+                nc.scalar.activation(
+                    out=head_squares[:], in_=u[:, head, :], func=SQUARE, accum_out=sum_sq[:, head : head + 1]
+                )
+            straight = stage.tile([P, HEADS_PER_BANK, HEAD], F32, name="straight")
+            nc.vector.tensor_tensor(
+                out=straight[:], in0=u[:], in1=cos_gain[:].unsqueeze(1).to_broadcast([P, HEADS_PER_BANK, HEAD]), op=MULT
+            )
+            turned = stage.tile([P, HEADS_PER_BANK, HEAD], F32, name="turned")
+            for here, other in ((slice(0, HALF), slice(HALF, HEAD)), (slice(HALF, HEAD), slice(0, HALF))):
+                nc.vector.tensor_tensor(
+                    out=turned[:, :, here],
+                    in0=u[:, :, other],
+                    in1=sin_gain[:, here].unsqueeze(1).to_broadcast([P, HEADS_PER_BANK, HALF]),
+                    op=MULT,
+                )
+            nc.vector.tensor_tensor(out=straight[:], in0=straight[:], in1=turned[:], op=ADD)
+            inv_rms_u = inverse_rms(nc, small, sum_sq[:], HEAD)
+            result = stage.tile([P, HEADS_PER_BANK, HEAD], F32, name="result")
+            for head in range(HEADS_PER_BANK):
+                nc.scalar.activation(
+                    out=result[:, head, :], in_=straight[:, head, :], func=COPY, scale=inv_rms_u[:, head : head + 1]
+                )
+            nc.gpsimd.dma_start(out=out_heads.rearrange("h t d -> t h d"), in_=result[:])
+
+        def heads_of(out, bank):
+            return out[0, bank * HEADS_PER_BANK : (bank + 1) * HEADS_PER_BANK]
+
+        q_sums = project(Wq_words, q_planes, N_Q)
+        for bank in range(N_Q // BANK):
+            norm_rope_store(q_sums[bank], q_tables, heads_of(out_0, bank))
+        k_sums = project(Wk_words, k_planes, N_K)
+        for bank in range(N_K // BANK):
+            norm_rope_store(k_sums[bank], k_tables, heads_of(out_1, bank))
+        v_sums = project(Wv_words, v_planes, N_V)
+        for bank in range(N_V // BANK):
+            v_sb = stage.tile([P, HEADS_PER_BANK, HEAD], F32, name="v_sb")
+            v_flat = v_sb[:].rearrange("p h d -> p (h d)")
+            if bank % 2 == 0:
+                nc.vector.tensor_copy(out=v_flat, in_=v_sums[bank][:])
+            else:
+                nc.scalar.copy(out=v_flat, in_=v_sums[bank][:])
+            nc.sync.dma_start(out=heads_of(out_2, bank).rearrange("h t d -> t h d"), in_=v_sb[:])

@@ -50,9 +50,9 @@ def load_scale_planes(nc, pool, w_scales, n, name):
     nc.vector.memset(planes[:].bitcast(I32), 0)
     for s in range(GROUPS // SHARED):
         for quad in range(P // QUADRANT):
-            nc.sync.dma_start(
-                out=planes[QUADRANT * quad : QUADRANT * quad + SHARED * PACK, s, :].bitcast(I32),
-                in_=w_scales[SHARED * s : SHARED * (s + 1), PACK * quad : PACK * (quad + 1), :].bitcast(I32),
+            nc.gpsimd.dma_start(
+                out=planes[QUADRANT * quad : QUADRANT * quad + SHARED * PACK, s, :].bitcast(F32),
+                in_=w_scales[SHARED * s : SHARED * (s + 1), PACK * quad : PACK * (quad + 1), :].bitcast(F32),
             )
     return planes
 

@@ -29,7 +29,7 @@ SHARED = 4
 QUADRANT = 32
 X_CHUNKS = 4
 LOAD_BYTES = 8192
-WORD_BUFFERS = 14
+WORD_BUFFERS = 12
 
 FLOPS = 2 * P * D * (N_Q + N_K + N_V)
 
@@ -93,6 +93,7 @@ def tile_rawkvinjector_pa_k_kernel(
         small = ctx.enter_context(tc.tile_pool(name="small", bufs=2))
         stage = ctx.enter_context(tc.tile_pool(name="stage", bufs=2))
         stream = ctx.enter_context(tc.tile_pool(name="stream", bufs=WORD_BUFFERS))
+        finished = ctx.enter_context(tc.tile_pool(name="finished", bufs=(N_Q + N_K) // BANK))
         psum = ctx.enter_context(tc.psum_pool(name="psum", bufs=8))
 
         x = keep.tile([P, D], BF16, name="x")
@@ -185,7 +186,7 @@ def tile_rawkvinjector_pa_k_kernel(
                         )
             return sums
 
-        def norm_rope_store(sums, tables, out_heads):
+        def norm_rope(sums, tables):
             cos_gain, sin_gain = tables
             u = stage.tile([P, HEADS_PER_BANK, HEAD], F32, name="u")
             nc.scalar.copy(out=u[:].rearrange("p h d -> p (h d)"), in_=sums[:])
@@ -209,23 +210,27 @@ def tile_rawkvinjector_pa_k_kernel(
                 )
             nc.vector.tensor_tensor(out=straight[:], in0=straight[:], in1=turned[:], op=ADD)
             inv_rms_u = inverse_rms(nc, small, sum_sq[:], HEAD)
-            result = stage.tile([P, HEADS_PER_BANK, HEAD], F32, name="result")
+            result = finished.tile([P, HEADS_PER_BANK, HEAD], F32, name="result")
             for head in range(HEADS_PER_BANK):
                 nc.scalar.activation(
                     out=result[:, head, :], in_=straight[:, head, :], func=COPY, scale=inv_rms_u[:, head : head + 1]
                 )
-            nc.gpsimd.dma_start(out=out_heads.rearrange("h t d -> t h d"), in_=result[:])
+            return result
 
-        def heads_of(out, bank):
-            return out[0, bank * HEADS_PER_BANK : (bank + 1) * HEADS_PER_BANK]
+        def store(out, bank, result):
+            heads = out[0, bank * HEADS_PER_BANK : (bank + 1) * HEADS_PER_BANK]
+            nc.sync.dma_start(out=heads.rearrange("h t d -> t h d"), in_=result[:])
 
         q_sums = project(Wq_words, q_planes, N_Q)
-        for bank in range(N_Q // BANK):
-            norm_rope_store(q_sums[bank], q_tables, heads_of(out_0, bank))
+        q_results = [norm_rope(sums, q_tables) for sums in q_sums]
         k_sums = project(Wk_words, k_planes, N_K)
-        for bank in range(N_K // BANK):
-            norm_rope_store(k_sums[bank], k_tables, heads_of(out_1, bank))
+        k_results = [norm_rope(sums, k_tables) for sums in k_sums]
         v_sums = project(Wv_words, v_planes, N_V)
+
+        for bank in range(N_Q // BANK):
+            store(out_0, bank, q_results[bank])
+        for bank in range(N_K // BANK):
+            store(out_1, bank, k_results[bank])
         for bank in range(N_V // BANK):
             v_sb = stage.tile([P, HEADS_PER_BANK, HEAD], F32, name="v_sb")
             v_flat = v_sb[:].rearrange("p h d -> p (h d)")
@@ -233,4 +238,4 @@ def tile_rawkvinjector_pa_k_kernel(
                 nc.vector.tensor_copy(out=v_flat, in_=v_sums[bank][:])
             else:
                 nc.scalar.copy(out=v_flat, in_=v_sums[bank][:])
-            nc.sync.dma_start(out=heads_of(out_2, bank).rearrange("h t d -> t h d"), in_=v_sb[:])
+            store(out_2, bank, v_sb)

@@ -27,6 +27,7 @@ N_Q, N_K, N_V = 2048, 1024, 1024
 EPS = 1e-6
 SHARED = 4
 QUADRANT = 32
+PLANE_ROWS = QUADRANT // 8
 X_CHUNKS = 4
 LOAD_BYTES = 8192
 WORD_BUFFERS = 12
@@ -48,11 +49,12 @@ def inverse_rms(nc, pool, sum_sq, count):
 def load_scale_planes(nc, pool, w_scales, n, name):
     planes = pool.tile([P, GROUPS // SHARED, n], U8, name=name, align_bytes=64)
     nc.vector.memset(planes[:].bitcast(I32), 0)
-    for s in range(GROUPS // SHARED):
+    for row in range(PLANE_ROWS):
         for quad in range(P // QUADRANT):
+            first = QUADRANT * quad + row
             nc.gpsimd.dma_start(
-                out=planes[QUADRANT * quad : QUADRANT * quad + SHARED * PACK, s, :].bitcast(F32),
-                in_=w_scales[SHARED * s : SHARED * (s + 1), PACK * quad : PACK * (quad + 1), :].bitcast(F32),
+                out=planes[first : first + SHARED * PLANE_ROWS : PLANE_ROWS, :, :].bitcast(F32),
+                in_=w_scales[:, PLANE_ROWS * quad + row, :].rearrange("(s j) n -> j s n", j=SHARED).bitcast(F32),
             )
     return planes
 
@@ -180,7 +182,7 @@ def tile_rawkvinjector_pa_k_kernel(
                             lhsT=h_codes[:, g * P : (g + 1) * P].bitcast(FP8X4),
                             lhsT_scale=h_planes[:, g * P : (g + 1) * P],
                             rhs=words[:, i, bank * BANK * PACK : (bank + 1) * BANK * PACK].bitcast(FP8X4),
-                            rhs_scale=planes[PACK * (g % SHARED) : P, g // SHARED, bank * BANK : (bank + 1) * BANK],
+                            rhs_scale=planes[PLANE_ROWS * (g % SHARED) : P, g // SHARED, bank * BANK : (bank + 1) * BANK],
                             start=(g == 0),
                             stop=(g == GROUPS - 1),
                         )

@@ -29,8 +29,8 @@ SHARED = 4
 QUADRANT = 32
 PLANE_ROWS = QUADRANT // 8
 X_CHUNKS = 4
-LOAD_BYTES = 8192
-WORD_BUFFERS = 12
+LOAD_BYTES = 16384
+WORD_BUFFERS = 6
 
 FLOPS = 2 * P * D * (N_Q + N_K + N_V)
 
@@ -165,16 +165,20 @@ def tile_rawkvinjector_pa_k_kernel(
         q_tables = rope_tables(nc, keep, head_gains[:, 0:HEAD], cos_sb, sin_sb, "q")
         k_tables = rope_tables(nc, keep, head_gains[:, HEAD : 2 * HEAD], cos_sb, sin_sb, "k")
 
-        def project(w_words, planes, n):
+        def project(w_words, planes, n, finer_end=False):
             sums = [psum.tile([P, BANK], F32, name="sums", tag="bank") for bank in range(n // BANK)]
             per_load = LOAD_BYTES // (n * PACK)
-            for first in range(0, GROUPS, per_load):
-                words = stream.tile([P, per_load, n * PACK], U8, name="words", align_bytes=64)
+            counts = [per_load] * (GROUPS // per_load)
+            if finer_end:
+                counts[-1:] = [per_load // 2, per_load // 2]
+            first = 0
+            for count in counts:
+                words = stream.tile([P, count, n * PACK], U8, name="words", align_bytes=64)
                 nc.sync.dma_start(
                     out=words[:].bitcast(I32),
-                    in_=w_words[first : first + per_load].rearrange("g p n t -> p g (n t)").bitcast(I32),
+                    in_=w_words[first : first + count].rearrange("g p n t -> p g (n t)").bitcast(I32),
                 )
-                for i in range(per_load):
+                for i in range(count):
                     g = first + i
                     for bank in range(n // BANK):
                         nc.tensor.matmul_mx(
@@ -186,6 +190,7 @@ def tile_rawkvinjector_pa_k_kernel(
                             start=(g == 0),
                             stop=(g == GROUPS - 1),
                         )
+                first += count
             return sums
 
         def norm_rope(sums, tables):
@@ -227,7 +232,7 @@ def tile_rawkvinjector_pa_k_kernel(
         q_results = [norm_rope(sums, q_tables) for sums in q_sums]
         k_sums = project(Wk_words, k_planes, N_K)
         k_results = [norm_rope(sums, k_tables) for sums in k_sums]
-        v_sums = project(Wv_words, v_planes, N_V)
+        v_sums = project(Wv_words, v_planes, N_V, finer_end=True)
 
         for bank in range(N_Q // BANK):
             store(out_0, bank, q_results[bank])

@@ -49,12 +49,12 @@ def inverse_rms(nc, pool, sum_sq, count):
 def load_scale_planes(nc, pool, w_scales, n, name):
     planes = pool.tile([P, GROUPS // SHARED, n], U8, name=name, align_bytes=64)
     nc.vector.memset(planes[:].bitcast(I32), 0)
-    for row in range(PLANE_ROWS):
+    for s in range(GROUPS // SHARED):
         for quad in range(P // QUADRANT):
-            first = QUADRANT * quad + row
+            first = QUADRANT * quad
             nc.gpsimd.dma_start(
-                out=planes[first : first + SHARED * PLANE_ROWS : PLANE_ROWS, :, :].bitcast(F32),
-                in_=w_scales[:, PLANE_ROWS * quad + row, :].rearrange("(s j) n -> j s n", j=SHARED).bitcast(F32),
+                out=planes[first : first + SHARED * PLANE_ROWS, s, :].bitcast(F32),
+                in_=w_scales[s * SHARED : (s + 1) * SHARED, PLANE_ROWS * quad : PLANE_ROWS * (quad + 1), :].bitcast(F32),
             )
     return planes
 
@@ -104,16 +104,16 @@ def tile_rawkvinjector_pa_k_kernel(
             cols = slice(c * chunk, (c + 1) * chunk)
             nc.sync.dma_start(out=x[:, cols], in_=hidden_states[0][:, cols])
 
-        cos_sb = keep.tile([P, HEAD], BF16, name="cos_sb")
-        nc.scalar.dma_start(out=cos_sb[:], in_=cos)
-        sin_sb = keep.tile([P, HEAD], BF16, name="sin_sb")
-        nc.scalar.dma_start(out=sin_sb[:], in_=sin)
-
         gains = keep.tile([P, D + 2 * HEAD], BF16, name="gains")
         nc.vector.memset(gains[:].bitcast(I32), 0)
         nc.scalar.dma_start(out=gains[0:1, 0:D], in_=ln1_w.unsqueeze(0))
         nc.scalar.dma_start(out=gains[0:1, D : D + HEAD], in_=q_norm_w.unsqueeze(0))
         nc.scalar.dma_start(out=gains[0:1, D + HEAD : D + 2 * HEAD], in_=k_norm_w.unsqueeze(0))
+        cos_sb = keep.tile([P, HEAD], BF16, name="cos_sb")
+        nc.scalar.dma_start(out=cos_sb[:], in_=cos)
+        sin_sb = keep.tile([P, HEAD], BF16, name="sin_sb")
+        nc.scalar.dma_start(out=sin_sb[:], in_=sin)
+
         ones = keep.tile([P, P], BF16, name="ones")
         nc.gpsimd.memset(ones[:], 1.0)
         ident = keep.tile([P, P], BF16, name="ident")
@@ -123,29 +123,30 @@ def tile_rawkvinjector_pa_k_kernel(
         k_planes = load_scale_planes(nc, keep, Wk_scales, N_K, "k_planes")
         v_planes = load_scale_planes(nc, keep, Wv_scales, N_V, "v_planes")
 
+        weighted = keep.tile([P, D], F32, name="weighted")
         chunk_sums = small.tile([P, X_CHUNKS], F32, name="chunk_sums")
         for c in range(X_CHUNKS):
             squares = stage.tile([P, chunk], BF16, name="squares")
             nc.scalar.activation(
                 out=squares[:], in_=x[:, c * chunk : (c + 1) * chunk], func=SQUARE, accum_out=chunk_sums[:, c : c + 1]
             )
-        row_sum = small.tile([P, 1], F32, name="row_sum")
-        nc.vector.tensor_reduce(out=row_sum[:], in_=chunk_sums[:], axis=mybir.AxisListType.X, op=ADD)
-        inv_rms_x = inverse_rms(nc, small, row_sum[:], D)
-
-        h = keep.tile([P, D], BF16, name="h")
         for g in range(GROUPS):
             cols = slice(g * GROUP, (g + 1) * GROUP)
             ln1_everywhere = psum.tile([P, GROUP], F32, name="ln1_everywhere", tag="bank")
             nc.tensor.matmul(out=ln1_everywhere[:], lhsT=ones[:], rhs=gains[:, cols], start=True, stop=True)
-            nc.vector.scalar_tensor_tensor(
-                out=h[:, cols], in0=x[:, cols], scalar=inv_rms_x[:, 0:1], in1=ln1_everywhere[:], op0=MULT, op1=MULT
-            )
+            nc.vector.tensor_tensor(out=weighted[:, cols], in0=x[:, cols], in1=ln1_everywhere[:], op=MULT)
+        row_sum = small.tile([P, 1], F32, name="row_sum")
+        nc.vector.tensor_reduce(out=row_sum[:], in_=chunk_sums[:], axis=mybir.AxisListType.X, op=ADD)
+        inv_rms_x = inverse_rms(nc, small, row_sum[:], D)
 
+        h = x
         h_codes = keep.tile([P, GROUPS * P], U32, name="h_codes", align_bytes=64)
         h_planes = keep.tile([P, GROUPS * P], U8, name="h_planes", align_bytes=64)
         pair = 2
-        for first in range(0, GROUPS, pair):
+
+        def turn(first):
+            cols = slice(first * GROUP, (first + pair) * GROUP)
+            nc.vector.tensor_scalar(out=h[:, cols], in0=weighted[:, cols], scalar1=inv_rms_x[:, 0:1], scalar2=None, op0=MULT)
             h_t = psum.tile([P, pair, PACK, P], BF16, name="h_t", tag="bank")
             for i in range(pair):
                 g = first + i
@@ -153,6 +154,9 @@ def tile_rawkvinjector_pa_k_kernel(
                     nc.tensor.transpose(h_t[:, i, t, :], h[:, g * GROUP + t : (g + 1) * GROUP : PACK], ident[:])
             grouped = stage.tile([P, pair, P, PACK], BF16, name="grouped", align_bytes=64)
             nc.scalar.copy(out=grouped[:], in_=h_t[:].rearrange("p i t r -> p i r t"))
+            return grouped
+
+        def quantise(first, grouped):
             cols = slice(first * P, (first + pair) * P)
             nc.vector.quantize_mx(
                 out=h_codes[:, cols].bitcast(FP8X4),
@@ -160,36 +164,37 @@ def tile_rawkvinjector_pa_k_kernel(
                 in_=grouped[:].rearrange("p i r t -> p (i r t)"),
             )
 
-        head_gains = psum.tile([P, 2 * HEAD], F32, name="head_gains", tag="bank")
-        nc.tensor.matmul(out=head_gains[:], lhsT=ones[:], rhs=gains[:, D : D + 2 * HEAD], start=True, stop=True)
-        q_tables = rope_tables(nc, keep, head_gains[:, 0:HEAD], cos_sb, sin_sb, "q")
-        k_tables = rope_tables(nc, keep, head_gains[:, HEAD : 2 * HEAD], cos_sb, sin_sb, "k")
+        def multiply(sums, w_words, planes, n, first, count):
+            words = stream.tile([P, count, n * PACK], U8, name="words", align_bytes=64)
+            nc.sync.dma_start(
+                out=words[:].bitcast(I32),
+                in_=w_words[first : first + count].rearrange("g p n t -> p g (n t)").bitcast(I32),
+            )
+            for i in range(count):
+                g = first + i
+                for bank in range(n // BANK):
+                    nc.tensor.matmul_mx(
+                        out=sums[bank][:],
+                        lhsT=h_codes[:, g * P : (g + 1) * P].bitcast(FP8X4),
+                        lhsT_scale=h_planes[:, g * P : (g + 1) * P],
+                        rhs=words[:, i, bank * BANK * PACK : (bank + 1) * BANK * PACK].bitcast(FP8X4),
+                        rhs_scale=planes[PLANE_ROWS * (g % SHARED) : P, g // SHARED, bank * BANK : (bank + 1) * BANK],
+                        start=(g == 0),
+                        stop=(g == GROUPS - 1),
+                    )
+
+        def new_sums(n):
+            return [psum.tile([P, BANK], F32, name="sums", tag="bank") for bank in range(n // BANK)]
 
         def project(w_words, planes, n, finer_end=False):
-            sums = [psum.tile([P, BANK], F32, name="sums", tag="bank") for bank in range(n // BANK)]
+            sums = new_sums(n)
             per_load = LOAD_BYTES // (n * PACK)
             counts = [per_load] * (GROUPS // per_load)
             if finer_end:
                 counts[-1:] = [per_load // 2, per_load // 2]
             first = 0
             for count in counts:
-                words = stream.tile([P, count, n * PACK], U8, name="words", align_bytes=64)
-                nc.sync.dma_start(
-                    out=words[:].bitcast(I32),
-                    in_=w_words[first : first + count].rearrange("g p n t -> p g (n t)").bitcast(I32),
-                )
-                for i in range(count):
-                    g = first + i
-                    for bank in range(n // BANK):
-                        nc.tensor.matmul_mx(
-                            out=sums[bank][:],
-                            lhsT=h_codes[:, g * P : (g + 1) * P].bitcast(FP8X4),
-                            lhsT_scale=h_planes[:, g * P : (g + 1) * P],
-                            rhs=words[:, i, bank * BANK * PACK : (bank + 1) * BANK * PACK].bitcast(FP8X4),
-                            rhs_scale=planes[PLANE_ROWS * (g % SHARED) : P, g // SHARED, bank * BANK : (bank + 1) * BANK],
-                            start=(g == 0),
-                            stop=(g == GROUPS - 1),
-                        )
+                multiply(sums, w_words, planes, n, first, count)
                 first += count
             return sums
 
@@ -228,7 +233,22 @@ def tile_rawkvinjector_pa_k_kernel(
             heads = out[0, bank * HEADS_PER_BANK : (bank + 1) * HEADS_PER_BANK]
             nc.sync.dma_start(out=heads.rearrange("h t d -> t h d"), in_=result[:])
 
-        q_sums = project(Wq_words, q_planes, N_Q)
+        q_sums = None
+        waiting = turn(0)
+        for first in range(0, GROUPS, pair):
+            turned = waiting
+            if first + pair < GROUPS:
+                waiting = turn(first + pair)
+            quantise(first, turned)
+            if q_sums is None:
+                q_sums = new_sums(N_Q)
+            multiply(q_sums, Wq_words, q_planes, N_Q, first, pair)
+
+        head_gains = psum.tile([P, 2 * HEAD], F32, name="head_gains", tag="bank")
+        nc.tensor.matmul(out=head_gains[:], lhsT=ones[:], rhs=gains[:, D : D + 2 * HEAD], start=True, stop=True)
+        q_tables = rope_tables(nc, keep, head_gains[:, 0:HEAD], cos_sb, sin_sb, "q")
+        k_tables = rope_tables(nc, keep, head_gains[:, HEAD : 2 * HEAD], cos_sb, sin_sb, "k")
+
         q_results = [norm_rope(sums, q_tables) for sums in q_sums]
         k_sums = project(Wk_words, k_planes, N_K)
         k_results = [norm_rope(sums, k_tables) for sums in k_sums]

@@ -27,8 +27,10 @@ N_Q, N_K, N_V = 2048, 1024, 1024
 EPS = 1e-6
 SHARED = 4
 QUADRANT = 32
+GAIN_ROW = 16
 PLANE_ROWS = QUADRANT // 8
-X_CHUNKS = 4
+X_CHUNKS = 2
+SQUARED = 2048
 LOAD_BYTES = 16384
 WORD_BUFFERS = 6
 
@@ -104,36 +106,44 @@ def tile_rawkvinjector_pa_k_kernel(
             cols = slice(c * chunk, (c + 1) * chunk)
             nc.sync.dma_start(out=x[:, cols], in_=hidden_states[0][:, cols])
 
-        gains = keep.tile([P, D + 2 * HEAD], BF16, name="gains")
+        gains = keep.tile([P, GROUP], BF16, name="gains")
         nc.vector.memset(gains[:].bitcast(I32), 0)
-        nc.scalar.dma_start(out=gains[0:1, 0:D], in_=ln1_w.unsqueeze(0))
-        nc.scalar.dma_start(out=gains[0:1, D : D + HEAD], in_=q_norm_w.unsqueeze(0))
-        nc.scalar.dma_start(out=gains[0:1, D + HEAD : D + 2 * HEAD], in_=k_norm_w.unsqueeze(0))
+        nc.scalar.dma_start(out=gains[GAIN_ROW : GAIN_ROW + GROUPS, :], in_=ln1_w.rearrange("(g c) -> g c", c=GROUP))
+        q_gain_row = GAIN_ROW + 2 * QUADRANT
+        k_gain_row = q_gain_row + 1
+        nc.scalar.dma_start(out=gains[q_gain_row : q_gain_row + 1, 0:HEAD], in_=q_norm_w.unsqueeze(0))
+        nc.scalar.dma_start(out=gains[k_gain_row : k_gain_row + 1, 0:HEAD], in_=k_norm_w.unsqueeze(0))
         cos_sb = keep.tile([P, HEAD], BF16, name="cos_sb")
         nc.scalar.dma_start(out=cos_sb[:], in_=cos)
         sin_sb = keep.tile([P, HEAD], BF16, name="sin_sb")
         nc.scalar.dma_start(out=sin_sb[:], in_=sin)
 
-        ones = keep.tile([P, P], BF16, name="ones")
-        nc.gpsimd.memset(ones[:], 1.0)
         ident = keep.tile([P, P], BF16, name="ident")
         make_identity(nc, ident[:])
+
+        def gain_everywhere(out, row, n):
+            nc.tensor.matmul(
+                out=out, lhsT=ident[:, row : row + 1].to_broadcast([P, P]), rhs=gains[:, 0:n], start=True, stop=True
+            )
 
         q_planes = load_scale_planes(nc, keep, Wq_scales, N_Q, "q_planes")
         k_planes = load_scale_planes(nc, keep, Wk_scales, N_K, "k_planes")
         v_planes = load_scale_planes(nc, keep, Wv_scales, N_V, "v_planes")
 
         weighted = keep.tile([P, D], F32, name="weighted")
-        chunk_sums = small.tile([P, X_CHUNKS], F32, name="chunk_sums")
-        for c in range(X_CHUNKS):
-            squares = stage.tile([P, chunk], BF16, name="squares")
+        chunk_sums = small.tile([P, D // SQUARED], F32, name="chunk_sums")
+        for c in range(D // SQUARED):
+            squares = stage.tile([P, SQUARED], BF16, name="squares")
             nc.scalar.activation(
-                out=squares[:], in_=x[:, c * chunk : (c + 1) * chunk], func=SQUARE, accum_out=chunk_sums[:, c : c + 1]
+                out=squares[:],
+                in_=x[:, c * SQUARED : (c + 1) * SQUARED],
+                func=SQUARE,
+                accum_out=chunk_sums[:, c : c + 1],
             )
         for g in range(GROUPS):
             cols = slice(g * GROUP, (g + 1) * GROUP)
             ln1_everywhere = psum.tile([P, GROUP], F32, name="ln1_everywhere", tag="bank")
-            nc.tensor.matmul(out=ln1_everywhere[:], lhsT=ones[:], rhs=gains[:, cols], start=True, stop=True)
+            gain_everywhere(ln1_everywhere[:], GAIN_ROW + g, GROUP)
             nc.vector.tensor_tensor(out=weighted[:, cols], in0=x[:, cols], in1=ln1_everywhere[:], op=MULT)
         row_sum = small.tile([P, 1], F32, name="row_sum")
         nc.vector.tensor_reduce(out=row_sum[:], in_=chunk_sums[:], axis=mybir.AxisListType.X, op=ADD)
@@ -245,7 +255,8 @@ def tile_rawkvinjector_pa_k_kernel(
             multiply(q_sums, Wq_words, q_planes, N_Q, first, pair)
 
         head_gains = psum.tile([P, 2 * HEAD], F32, name="head_gains", tag="bank")
-        nc.tensor.matmul(out=head_gains[:], lhsT=ones[:], rhs=gains[:, D : D + 2 * HEAD], start=True, stop=True)
+        gain_everywhere(head_gains[:, 0:HEAD], q_gain_row, HEAD)
+        gain_everywhere(head_gains[:, HEAD : 2 * HEAD], k_gain_row, HEAD)
         q_tables = rope_tables(nc, keep, head_gains[:, 0:HEAD], cos_sb, sin_sb, "q")
         k_tables = rope_tables(nc, keep, head_gains[:, HEAD : 2 * HEAD], cos_sb, sin_sb, "k")
 

from contextlib import ExitStack

import concourse.mybir as mybir
from concourse.masks import make_identity

BF16 = mybir.dt.bfloat16
F32 = mybir.dt.float32
I32 = mybir.dt.int32
U8 = mybir.dt.uint8
U32 = mybir.dt.uint32
FP8X4 = mybir.dt.float8_e4m3fn_x4
MULT = mybir.AluOpType.mult
ADD = mybir.AluOpType.add
SQUARE = mybir.ActivationFunctionType.Square
COPY = mybir.ActivationFunctionType.Copy

P = 128
D = 8192
PACK = 4
GROUP = P * PACK
GROUPS = D // GROUP
HEAD = 128
HALF = HEAD // 2
BANK = 512
HEADS_PER_BANK = BANK // HEAD
N_Q, N_K, N_V = 2048, 1024, 1024
EPS = 1e-6
SHARED = 4
QUADRANT = 32
GAIN_ROW = 16
PLANE_ROWS = QUADRANT // 8
X_CHUNKS = 2
SQUARED = 2048
LOAD_BYTES = 16384
WORD_BUFFERS = 6

FLOPS = 2 * P * D * (N_Q + N_K + N_V)


def inverse_rms(nc, pool, sum_sq, count):
    width = sum_sq.shape[1]
    mean_sq = pool.tile([P, width], F32, name="mean_sq")
    nc.vector.tensor_scalar(out=mean_sq[:], in0=sum_sq, scalar1=1.0 / count, scalar2=EPS, op0=MULT, op1=ADD)
    rms = pool.tile([P, width], F32, name="rms")
    nc.scalar.sqrt(rms[:], mean_sq[:])
    inv = pool.tile([P, width], F32, name="inv")
    nc.vector.reciprocal(inv[:], rms[:])
    return inv


def load_scale_planes(nc, pool, w_scales, n, name):
    planes = pool.tile([P, GROUPS // SHARED, n], U8, name=name, align_bytes=64)
    nc.vector.memset(planes[:].bitcast(I32), 0)
    for s in range(GROUPS // SHARED):
        for quad in range(P // QUADRANT):
            first = QUADRANT * quad
            nc.gpsimd.dma_start(
                out=planes[first : first + SHARED * PLANE_ROWS, s, :].bitcast(F32),
                in_=w_scales[s * SHARED : (s + 1) * SHARED, PLANE_ROWS * quad : PLANE_ROWS * (quad + 1), :].bitcast(F32),
            )
    return planes


def rope_tables(nc, pool, gain, cos_sb, sin_sb, name):
    cos_gain = pool.tile([P, HEAD], F32, name=name + "_cos_gain")
    nc.vector.tensor_tensor(out=cos_gain[:], in0=gain, in1=cos_sb[:], op=MULT)
    sin_gain = pool.tile([P, HEAD], F32, name=name + "_sin_gain")
    nc.vector.scalar_tensor_tensor(
        out=sin_gain[:, 0:HALF], in0=gain[:, HALF:HEAD], scalar=-1.0, in1=sin_sb[:, 0:HALF], op0=MULT, op1=MULT
    )
    nc.vector.tensor_tensor(out=sin_gain[:, HALF:HEAD], in0=gain[:, 0:HALF], in1=sin_sb[:, HALF:HEAD], op=MULT)
    return cos_gain, sin_gain


def tile_rawkvinjector_pa_k_kernel(
    tc,
    hidden_states,
    ln1_w,
    Wq_words,
    Wq_scales,
    Wk_words,
    Wk_scales,
    Wv_words,
    Wv_scales,
    q_norm_w,
    k_norm_w,
    cos,
    sin,
    out_0,
    out_1,
    out_2,
):
    nc = tc.nc
    with ExitStack() as ctx:
        ctx.enter_context(tc.manual_schedule())
        keep = ctx.enter_context(tc.tile_pool(name="keep", bufs=1))
        small = ctx.enter_context(tc.tile_pool(name="small", bufs=2))
        stage = ctx.enter_context(tc.tile_pool(name="stage", bufs=2))
        stream = ctx.enter_context(tc.tile_pool(name="stream", bufs=WORD_BUFFERS))
        finished = ctx.enter_context(tc.tile_pool(name="finished", bufs=(N_Q + N_K) // BANK))
        psum = ctx.enter_context(tc.psum_pool(name="psum", bufs=8))

        x = keep.tile([P, D], BF16, name="x")
        chunk = D // X_CHUNKS
        for c in range(X_CHUNKS):
            cols = slice(c * chunk, (c + 1) * chunk)
            nc.sync.dma_start(out=x[:, cols], in_=hidden_states[0][:, cols])

        gains = keep.tile([P, GROUP], BF16, name="gains")
        nc.vector.memset(gains[:].bitcast(I32), 0)
        nc.scalar.dma_start(out=gains[GAIN_ROW : GAIN_ROW + GROUPS, :], in_=ln1_w.rearrange("(g c) -> g c", c=GROUP))
        q_gain_row = GAIN_ROW + 2 * QUADRANT
        k_gain_row = q_gain_row + 1
        nc.scalar.dma_start(out=gains[q_gain_row : q_gain_row + 1, 0:HEAD], in_=q_norm_w.unsqueeze(0))
        nc.scalar.dma_start(out=gains[k_gain_row : k_gain_row + 1, 0:HEAD], in_=k_norm_w.unsqueeze(0))
        cos_sb = keep.tile([P, HEAD], BF16, name="cos_sb")
        nc.scalar.dma_start(out=cos_sb[:], in_=cos)
        sin_sb = keep.tile([P, HEAD], BF16, name="sin_sb")
        nc.scalar.dma_start(out=sin_sb[:], in_=sin)

        ident = keep.tile([P, P], BF16, name="ident")
        make_identity(nc, ident[:])

        def gain_everywhere(out, row, n):
            nc.tensor.matmul(
                out=out, lhsT=ident[:, row : row + 1].to_broadcast([P, P]), rhs=gains[:, 0:n], start=True, stop=True
            )

        q_planes = load_scale_planes(nc, keep, Wq_scales, N_Q, "q_planes")
        k_planes = load_scale_planes(nc, keep, Wk_scales, N_K, "k_planes")
        v_planes = load_scale_planes(nc, keep, Wv_scales, N_V, "v_planes")

        weighted = keep.tile([P, D], F32, name="weighted")
        chunk_sums = small.tile([P, D // SQUARED], F32, name="chunk_sums")
        for c in range(D // SQUARED):
            squares = stage.tile([P, SQUARED], BF16, name="squares")
            nc.scalar.activation(
                out=squares[:],
                in_=x[:, c * SQUARED : (c + 1) * SQUARED],
                func=SQUARE,
                accum_out=chunk_sums[:, c : c + 1],
            )
        for g in range(GROUPS):
            cols = slice(g * GROUP, (g + 1) * GROUP)
            ln1_everywhere = psum.tile([P, GROUP], F32, name="ln1_everywhere", tag="bank")
            gain_everywhere(ln1_everywhere[:], GAIN_ROW + g, GROUP)
            nc.vector.tensor_tensor(out=weighted[:, cols], in0=x[:, cols], in1=ln1_everywhere[:], op=MULT)
        row_sum = small.tile([P, 1], F32, name="row_sum")
        nc.vector.tensor_reduce(out=row_sum[:], in_=chunk_sums[:], axis=mybir.AxisListType.X, op=ADD)
        inv_rms_x = inverse_rms(nc, small, row_sum[:], D)

        h = x
        h_codes = keep.tile([P, GROUPS * P], U32, name="h_codes", align_bytes=64)
        h_planes = keep.tile([P, GROUPS * P], U8, name="h_planes", align_bytes=64)
        pair = 2

        def turn(first):
            cols = slice(first * GROUP, (first + pair) * GROUP)
            nc.vector.tensor_scalar(out=h[:, cols], in0=weighted[:, cols], scalar1=inv_rms_x[:, 0:1], scalar2=None, op0=MULT)
            h_t = psum.tile([P, pair, PACK, P], BF16, name="h_t", tag="bank")
            for i in range(pair):
                g = first + i
                for t in range(PACK):
                    nc.tensor.transpose(h_t[:, i, t, :], h[:, g * GROUP + t : (g + 1) * GROUP : PACK], ident[:])
            grouped = stage.tile([P, pair, P, PACK], BF16, name="grouped", align_bytes=64)
            nc.scalar.copy(out=grouped[:], in_=h_t[:].rearrange("p i t r -> p i r t"))
            return grouped

        def quantise(first, grouped):
            cols = slice(first * P, (first + pair) * P)
            nc.vector.quantize_mx(
                out=h_codes[:, cols].bitcast(FP8X4),
                scales=h_planes[:, cols],
                in_=grouped[:].rearrange("p i r t -> p (i r t)"),
            )

        def multiply(sums, w_words, planes, n, first, count):
            words = stream.tile([P, count, n * PACK], U8, name="words", align_bytes=64)
            nc.sync.dma_start(
                out=words[:].bitcast(I32),
                in_=w_words[first : first + count].rearrange("g p n t -> p g (n t)").bitcast(I32),
            )
            for i in range(count):
                g = first + i
                for bank in range(n // BANK):
                    nc.tensor.matmul_mx(
                        out=sums[bank][:],
                        lhsT=h_codes[:, g * P : (g + 1) * P].bitcast(FP8X4),
                        lhsT_scale=h_planes[:, g * P : (g + 1) * P],
                        rhs=words[:, i, bank * BANK * PACK : (bank + 1) * BANK * PACK].bitcast(FP8X4),
                        rhs_scale=planes[PLANE_ROWS * (g % SHARED) : P, g // SHARED, bank * BANK : (bank + 1) * BANK],
                        start=(g == 0),
                        stop=(g == GROUPS - 1),
                    )

        def new_sums(n):
            return [psum.tile([P, BANK], F32, name="sums", tag="bank") for bank in range(n // BANK)]

        def project(w_words, planes, n, finer_end=False):
            sums = new_sums(n)
            per_load = LOAD_BYTES // (n * PACK)
            counts = [per_load] * (GROUPS // per_load)
            if finer_end:
                counts[-1:] = [per_load // 2, per_load // 2]
            first = 0
            for count in counts:
                multiply(sums, w_words, planes, n, first, count)
                first += count
            return sums

        def norm_rope(sums, tables):
            cos_gain, sin_gain = tables
            u = stage.tile([P, HEADS_PER_BANK, HEAD], F32, name="u")
            nc.scalar.copy(out=u[:].rearrange("p h d -> p (h d)"), in_=sums[:])
            sum_sq = small.tile([P, HEADS_PER_BANK], F32, name="sum_sq")
            for head in range(HEADS_PER_BANK):
                head_squares = stage.tile([P, HEAD], F32, name="head_squares")
                nc.scalar.activation(
                    out=head_squares[:], in_=u[:, head, :], func=SQUARE, accum_out=sum_sq[:, head : head + 1]
                )
            straight = stage.tile([P, HEADS_PER_BANK, HEAD], F32, name="straight")
            nc.vector.tensor_tensor(
                out=straight[:], in0=u[:], in1=cos_gain[:].unsqueeze(1).to_broadcast([P, HEADS_PER_BANK, HEAD]), op=MULT
            )
            turned = stage.tile([P, HEADS_PER_BANK, HEAD], F32, name="turned")
            for here, other in ((slice(0, HALF), slice(HALF, HEAD)), (slice(HALF, HEAD), slice(0, HALF))):
                nc.vector.tensor_tensor(
                    out=turned[:, :, here],
                    in0=u[:, :, other],
                    in1=sin_gain[:, here].unsqueeze(1).to_broadcast([P, HEADS_PER_BANK, HALF]),
                    op=MULT,
                )
            nc.vector.tensor_tensor(out=straight[:], in0=straight[:], in1=turned[:], op=ADD)
            inv_rms_u = inverse_rms(nc, small, sum_sq[:], HEAD)
            result = finished.tile([P, HEADS_PER_BANK, HEAD], F32, name="result")
            for head in range(HEADS_PER_BANK):
                nc.scalar.activation(
                    out=result[:, head, :], in_=straight[:, head, :], func=COPY, scale=inv_rms_u[:, head : head + 1]
                )
            return result

        def store(out, bank, result):
            heads = out[0, bank * HEADS_PER_BANK : (bank + 1) * HEADS_PER_BANK]
            nc.sync.dma_start(out=heads.rearrange("h t d -> t h d"), in_=result[:])

        q_sums = None
        waiting = turn(0)
        for first in range(0, GROUPS, pair):
            turned = waiting
            if first + pair < GROUPS:
                waiting = turn(first + pair)
            quantise(first, turned)
            if q_sums is None:
                q_sums = new_sums(N_Q)
            multiply(q_sums, Wq_words, q_planes, N_Q, first, pair)

        head_gains = psum.tile([P, 2 * HEAD], F32, name="head_gains", tag="bank")
        gain_everywhere(head_gains[:, 0:HEAD], q_gain_row, HEAD)
        gain_everywhere(head_gains[:, HEAD : 2 * HEAD], k_gain_row, HEAD)
        q_tables = rope_tables(nc, keep, head_gains[:, 0:HEAD], cos_sb, sin_sb, "q")
        k_tables = rope_tables(nc, keep, head_gains[:, HEAD : 2 * HEAD], cos_sb, sin_sb, "k")

        q_results = [norm_rope(sums, q_tables) for sums in q_sums]
        k_sums = project(Wk_words, k_planes, N_K)
        k_results = [norm_rope(sums, k_tables) for sums in k_sums]
        v_sums = project(Wv_words, v_planes, N_V, finer_end=True)

        for bank in range(N_Q // BANK):
            store(out_0, bank, q_results[bank])
        for bank in range(N_K // BANK):
            store(out_1, bank, k_results[bank])
        for bank in range(N_V // BANK):
            v_sb = stage.tile([P, HEADS_PER_BANK, HEAD], F32, name="v_sb")
            v_flat = v_sb[:].rearrange("p h d -> p (h d)")
            if bank % 2 == 0:
                nc.vector.tensor_copy(out=v_flat, in_=v_sums[bank][:])
            else:
                nc.scalar.copy(out=v_flat, in_=v_sums[bank][:])
            store(out_2, bank, v_sb)
